import numpy as np
import ml_dtypes


def mxq(x, axis, fmt="e4m3"):
    dtype, down = {"e4m3": (ml_dtypes.float8_e4m3fn, 7), "e5m2": (ml_dtypes.float8_e5m2, 14)}[fmt]
    v = np.moveaxis(np.asarray(x, np.float32).astype(ml_dtypes.bfloat16).astype(np.float64), axis, -1)
    blocks = v.reshape(v.shape[:-1] + (-1, 32))
    amax = np.abs(blocks).max(-1, keepdims=True)
    byte = np.maximum(np.where(amax > 0, np.frexp(amax)[1] - 1 + 127, 0) - down, 1)
    scale = np.exp2(byte - 127.0)
    codes = (blocks / scale).astype(np.float32).astype(dtype).astype(np.float64)
    return np.moveaxis((codes * scale).reshape(v.shape), -1, axis)


WIDE = False


def mx_kscale(k):
    if not WIDE:
        return np.ones(k)
    levels = np.array([10, -10, 5, -5, 0])
    if k % 512:
        return np.exp2(np.random.permutation(np.resize(levels, k // 32))).repeat(32)
    a = np.empty((k // 512, 16))
    for p in range(k // 512):
        a[p, :8] = np.random.permutation(np.resize(levels, 8))
        for g in range(8):
            far = levels[np.abs(levels - a[p, g]) >= 10]
            a[p, g + 8] = far[np.random.randint(len(far))]
    return np.exp2(a.ravel()).repeat(32)


BF16 = ml_dtypes.bfloat16


def bf(x):
    return np.asarray(x, np.float32).astype(BF16)


def f64(x):
    return np.asarray(x).astype(np.float64)


B, S, D, H, QL, KL, ND, VD, RD = 4, 1024, 1024, 4, 512, 512, 64, 128, 64
QH = ND + RD
BASE = 10000.0


def rope(v):
    d = v.shape[-1]
    inv_freq = BASE ** (-np.arange(0, d, 2) / d)
    ang = np.arange(v.shape[1])[:, None] * inv_freq[None, :]
    cos = np.cos(ang)[None, :, None, :]
    sin = np.sin(ang)[None, :, None, :]
    v1 = v[..., 0::2]
    v2 = v[..., 1::2]
    o1 = v1 * cos - v2 * sin
    o2 = v1 * sin + v2 * cos
    return np.stack([o1, o2], axis=-1).reshape(v.shape)


def draw0():
    s, t = mx_kscale(D), mx_kscale(QL)
    return {"x": bf(np.random.standard_normal((B, S, D)) * s),
            "Wqa": bf(np.random.standard_normal((D, QL)) / np.sqrt(D) / s[:, None] * t),
            "Wqb": bf(np.random.standard_normal((QL, H * QH)) / np.sqrt(QL) / t[:, None])}


def core(x, Wqa, Wqb):
    cq = mxq(f64(x), 2, "e4m3") @ mxq(f64(Wqa), 0, "e4m3")
    q = (mxq(cq, 2, "e4m3") @ mxq(f64(Wqb), 0, "e4m3")).reshape(B, S, H, QH)
    q_nope, q_pe = q[..., :ND], q[..., ND:]
    return np.concatenate([q_nope, rope(q_pe)], axis=-1)


def e4m3fn_bytes(y):
    return np.clip(np.asarray(y, np.float64), -448.0, 448.0).astype(np.float32).astype(ml_dtypes.float8_e4m3fn).view(np.uint8)


def e4m3fn_values(b):
    return np.asarray(b, np.uint8).view(ml_dtypes.float8_e4m3fn).astype(np.float64)


def setup_inputs():
    d = draw0()
    x0 = np.asarray(d['x']).astype(np.float64)
    s = (np.max(np.abs(x0), axis=(0, 1), keepdims=True) / 448.0).astype(np.float32)
    out = {}
    for k, v in d.items():
        if k == 'x':
            out['x_bytes'] = e4m3fn_bytes(x0 / s.astype(np.float64))
            out['x_scale'] = s
        else:
            out[k] = v
    return out


def reference(x_bytes, x_scale, Wqa, Wqb):
    return core(e4m3fn_values(x_bytes) * x_scale.astype(np.float64), Wqa, Wqb)

import math

import concourse.mybir as mybir
from concourse.masks import make_identity

F32 = mybir.dt.float32
BF16 = mybir.dt.bfloat16
U32 = mybir.dt.uint32
U8 = mybir.dt.uint8
I32 = mybir.dt.int32
FP8 = mybir.dt.float8_e4m3fn
FP8X4 = mybir.dt.float8_e4m3fn_x4
ALU = mybir.AluOpType
ACT = mybir.ActivationFunctionType

P = 128
TOKENS, D, QL, OUT = 4096, 1024, 512, 512
HEADS, PLAIN, ROT = 4, 64, 64
PAIRS = ROT // 2
BASE = 10000.0
FLOPS = 2 * TOKENS * D * QL + 2 * TOKENS * QL * OUT

UNIT = 2 * P
UNITS = TOKENS // UNIT


def tile_multilatentattention_pa_t_kernel(tc, x_bytes, x_scale, Wqa, Wqb, out):
    nc = tc.nc
    x_v = x_bytes.flatten_outer_dims().rearrange("(q p i) k -> q p (i k)", p=P, i=4)
    o_v = out.rearrange("b s h d -> (b s) (h d)").rearrange("(q p i) f -> q p (i f)", p=P, i=4)
    wa_v = Wqa.rearrange("(g p j) c -> g p (j c)", p=P, j=4)
    wb_v = Wqb.rearrange("(p j) c -> p (j c)", j=4)

    with (
        tc.tile_pool(name="keep", bufs=1) as keep,
        tc.tile_pool(name="stream", bufs=4) as stream,
        tc.tile_pool(name="mid", bufs=3) as mid,
        tc.psum_pool(name="ps_x", bufs=4) as ps_x,
        tc.psum_pool(name="ps_c", bufs=2) as ps_c,
        tc.psum_pool(name="ps_q", bufs=2) as ps_q,
        tc.manual_schedule(),
    ):
        xsc = keep.tile([P, 2, 4], F32, name="xsc")
        nc.scalar.dma_start(out=xsc[:], in_=x_scale.rearrange("a b (g p t) -> p (a b g) t", p=P, t=4))
        wa_raw = [keep.tile([P, 2048], BF16, name=f"wa_raw{g}") for g in range(2)]
        wb_raw = keep.tile([P, 2048], BF16, name="wb_raw")
        xb = []
        for q in range(8):
            t = keep.tile([P, 4096], U8, name=f"xb{q}")
            xb.append(t)
        nc.sync.dma_start(out=xb[0][:, 0:2048], in_=x_v[0][:, 0:2048])
        nc.sync.dma_start(out=wa_raw[0][:], in_=wa_v[0])
        nc.sync.dma_start(out=xb[0][:, 2048:4096], in_=x_v[0][:, 2048:4096])
        nc.sync.dma_start(out=wa_raw[1][:], in_=wa_v[1])
        nc.sync.dma_start(out=wb_raw[:], in_=wb_v)
        for q in range(1, 8):
            nc.sync.dma_start(out=xb[q][:], in_=x_v[q])

        ident = keep.tile([P, P], F32, name="ident")
        make_identity(nc, ident[:])
        pos = keep.tile([P, 8], F32, name="pos")
        nc.gpsimd.iota(pos[:], [[512, 2], [1, 4]], base=0, channel_multiplier=4, allow_small_or_imprecise_dtypes=True)
        one = keep.tile([P, 1], F32, name="one")
        nc.gpsimd.memset(one[:], 1.0)
        freq = keep.tile([P, PAIRS], F32, name="freq")
        nc.gpsimd.tensor_scalar(out=freq[:, 0:1], in0=one[:], scalar1=1.0 / (2.0 * math.pi), scalar2=0.0, op0=ALU.mult, op1=ALU.add)
        w = 1
        while w < PAIRS:
            nc.gpsimd.tensor_scalar(out=freq[:, w : 2 * w], in0=freq[:, 0:w], scalar1=BASE ** (-w / PAIRS), scalar2=0.0, op0=ALU.mult, op1=ALU.add)
            w *= 2
        turns = keep.tile([P, 2, 8, PAIRS], F32, name="turns")
        nc.gpsimd.tensor_tensor(
            out=turns[:, 0],
            in0=pos[:].unsqueeze(2).to_broadcast([P, 8, PAIRS]),
            in1=freq[:].unsqueeze(1).to_broadcast([P, 8, PAIRS]),
            op=ALU.mult,
        )
        nc.gpsimd.tensor_scalar(out=turns[:, 1], in0=turns[:, 0], scalar1=1.0, scalar2=0.25, op0=ALU.mult, op1=ALU.add)
        whole_i = keep.tile([P, 2, 8, PAIRS], I32, name="whole_i")
        whole_f = keep.tile([P, 2, 8, PAIRS], F32, name="whole_f")
        nc.vector.tensor_copy(out=whole_i[:], in_=turns[:])
        nc.vector.tensor_copy(out=whole_f[:], in_=whole_i[:])
        frac = keep.tile([P, 2, 8, PAIRS], F32, name="frac")
        nc.gpsimd.tensor_tensor(out=frac[:], in0=turns[:], in1=whole_f[:], op=ALU.subtract)
        sines = keep.tile([P, 3, 8, PAIRS], F32, name="sines")
        trig = keep.tile([P, 8, 2, ROT], F32, name="trig")

        wa_g = [keep.tile([P, 2048], BF16, name=f"wa_g{g}", align_bytes=64) for g in range(2)]
        wa_c = [keep.tile([P, QL], U32, name=f"wa_c{g}", align_bytes=64) for g in range(2)]
        wa_s = [keep.tile([P, QL], U8, name=f"wa_s{g}", align_bytes=64) for g in range(2)]
        wb_g = keep.tile([P, 2048], BF16, name="wb_g", align_bytes=64)
        wb_c = keep.tile([P, OUT], U32, name="wb_c", align_bytes=64)
        wb_s = keep.tile([P, OUT], U8, name="wb_s", align_bytes=64)

        def wa_views(g):
            return (
                wa_g[g][:].rearrange("p (t m j) -> p t m j", t=4, j=4),
                wa_raw[g][:].rearrange("p (j m t) -> p t m j", j=4, t=4),
            )

        def quant(codes, scales, src):
            nc.vector.quantize_mx(out=codes[:].bitcast(FP8X4), scales=scales[:], in_=src[:])

        live = {}

        def widen(u):
            if not 0 <= u < UNITS:
                return
            xw = stream.tile([P, 2048], BF16, name="xw")
            src = xb[u // 2][:, (u % 2) * 2048 : (u % 2) * 2048 + 2048].bitcast(FP8)
            nc.scalar.copy(out=xw[:], in_=src)
            live["xw", u] = xw

        def turn(u):
            if not 0 <= u < UNITS:
                return
            words = live["xw", u][:].bitcast(F32)
            for g in range(2):
                xt = ps_x.tile([P, 2, 2, P], F32, name="xt")
                for i in range(2):
                    for e in range(2):
                        a = 512 * i + 256 * g
                        nc.tensor.transpose(xt[:, e, i, :], words[:, a + e : a + 256 : 2], ident[:])
                live["xt", u, g] = xt

        def scale_x(u, g):
            if not 0 <= u < UNITS:
                return
            if g == 0:
                xq = mid.tile([P, 2048], BF16, name="xq", align_bytes=64)
                live["xq", u] = xq
            xq = live["xq", u]
            src = live["xt", u, g][:].rearrange("p u i r -> p (u i r)").bitcast(BF16).rearrange("p (u n e) -> p n u e", u=2, e=2)
            nc.vector.tensor_tensor(
                out=xq[:, g * 1024 : (g + 1) * 1024].rearrange("p (n u e) -> p n u e", u=2, e=2),
                in0=src,
                in1=xsc[:, g, :].rearrange("p (u e) -> p u e", u=2).unsqueeze(1).to_broadcast([P, UNIT, 2, 2]),
                op=ALU.mult,
            )

        def quant_x(u):
            if not 0 <= u < UNITS:
                return
            xc = mid.tile([P, 512], U32, name="xc", align_bytes=64)
            xs = mid.tile([P, 512], U8, name="xs", align_bytes=64)
            quant(xc, xs, live["xq", u])
            live["xc", u] = (xc, xs)

        def stage1(u):
            if not 0 <= u < UNITS:
                return
            xc, xs = live["xc", u]
            for i in range(2):
                cq = ps_c.tile([P, 512], F32, name="cq")
                for t in range(4):
                    for g in range(2):
                        a = g * UNIT + i * P
                        nc.tensor.matmul_mx(
                            out=cq[:, t * P : (t + 1) * P],
                            lhsT=wa_c[g][:, t * P : (t + 1) * P].bitcast(FP8X4),
                            lhsT_scale=wa_s[g][:, t * P : (t + 1) * P],
                            rhs=xc[:, a : a + P].bitcast(FP8X4),
                            rhs_scale=xs[:, a : a + P],
                            start=(g == 0),
                            stop=(g == 1),
                        )
                live["cq", u, i] = cq

        def gather_cq(u, i, copy):
            if not 0 <= u < UNITS:
                return
            if i == 0:
                cb = mid.tile([P, 1024], BF16, name="cb", align_bytes=64)
                live["cb", u] = cb
            cb = live["cb", u]
            copy(
                out=cb[:, i * 512 : (i + 1) * 512].rearrange("p (n t) -> p n t", t=4),
                in_=live["cq", u, i][:].rearrange("p (t n) -> p n t", t=4),
            )

        def quant_c(u):
            if not 0 <= u < UNITS:
                return
            cc = mid.tile([P, 256], U32, name="cc", align_bytes=64)
            cs = mid.tile([P, 256], U8, name="cs", align_bytes=64)
            quant(cc, cs, live["cb", u])
            live["cc", u] = (cc, cs)

        def stage2(u):
            if not 0 <= u < UNITS:
                return
            cc, cs = live["cc", u]
            for i in range(2):
                qt = ps_q.tile([P, OUT], F32, name="qt")
                nc.tensor.matmul_mx(
                    out=qt[:],
                    lhsT=cc[:, i * P : (i + 1) * P].bitcast(FP8X4),
                    lhsT_scale=cs[:, i * P : (i + 1) * P],
                    rhs=wb_c[:].bitcast(FP8X4),
                    rhs_scale=wb_s[:],
                    start=True,
                    stop=True,
                )
                live["qt", u, i] = qt
            ot = stream.tile([P, 2, OUT], F32, name="ot")
            live["ot", u] = ot

        def heads(ap):
            return ap.rearrange("p (h f) -> p h f", h=HEADS)

        def take_all(u, i):
            if not 0 <= u < UNITS:
                return
            nc.scalar.copy(out=live["ot", u][:, i, :], in_=live["qt", u, i][:])

        def take_plain(u, i):
            if not 0 <= u < UNITS:
                return
            nc.scalar.copy(out=heads(live["ot", u][:, i, :])[:, :, 0:PLAIN], in_=heads(live["qt", u, i][:])[:, :, 0:PLAIN])

        def products(u, i, eng, src):
            if not 0 <= u < UNITS:
                return
            ci = (u // 2) % 2 * 4 + (u % 2) * 2 + i
            pr = mid.tile([P, 2, HEADS, ROT], F32, name=f"pr{i}")
            q_rot = heads(src)[:, :, PLAIN:]
            eng.tensor_tensor(
                out=pr[:],
                in0=q_rot.unsqueeze(1).to_broadcast([P, 2, HEADS, ROT]),
                in1=trig[:, ci].unsqueeze(2).to_broadcast([P, 2, HEADS, ROT]),
                op=ALU.mult,
            )
            live["pr", u, i] = pr

        def sums(u, i, eng):
            if not 0 <= u < UNITS:
                return
            pr = live["pr", u, i][:].rearrange("p s h (j e) -> p h j s e", e=2)
            eng.tensor_tensor(
                out=heads(live["ot", u][:, i, :])[:, :, PLAIN:].rearrange("p h (j s) -> p h j s", s=2),
                in0=pr[:, :, :, :, 0],
                in1=pr[:, :, :, :, 1],
                op=ALU.add,
            )

        def store(u):
            if not 0 <= u < UNITS:
                return
            half = (u % 2) * 1024
            nc.sync.dma_start(out=o_v[u // 2][:, half : half + 1024], in_=live["ot", u][:].rearrange("p i f -> p (i f)"))

        widen(0)
        turn(0)
        w_out, w_in = wa_views(0)
        nc.vector.tensor_copy(out=w_out, in_=w_in)
        widen(1)
        turn(1)
        nc.scalar.activation(out=sines[:, 0:2], in_=frac[:], func=ACT.Sin, scale=2.0 * math.pi)
        nc.scalar.activation(out=sines[:, 2], in_=frac[:, 0], func=ACT.Sin, scale=-2.0 * math.pi)
        w_out, w_in = wa_views(1)
        nc.scalar.copy(out=w_out, in_=w_in)
        for s in range(2):
            k = 1 - s
            nc.gpsimd.tensor_scalar(
                out=trig[:, :, s].rearrange("p c (j e) -> p c j e", e=2),
                in0=sines[:, k : k + 2].rearrange("p e c j -> p c j e"),
                scalar1=1.0, scalar2=0.0, op0=ALU.mult, op1=ALU.add,
            )
        nc.gpsimd.tensor_scalar(
            out=wb_g[:].rearrange("p (c j) -> p c j", j=4),
            in0=wb_raw[:].rearrange("p (j c) -> p c j", j=4),
            scalar1=1.0, scalar2=0.0, op0=ALU.mult, op1=ALU.add,
        )
        scale_x(0, 0)
        quant(wa_c[0], wa_s[0], wa_g[0])
        scale_x(0, 1)
        widen(2)
        scale_x(1, 0)
        quant_x(0)
        quant(wa_c[1], wa_s[1], wa_g[1])
        stage1(0)
        turn(2)
        scale_x(1, 1)
        gather_cq(0, 0, nc.scalar.copy)
        gather_cq(0, 1, nc.scalar.copy)
        quant(wb_c, wb_s, wb_g)
        quant_x(1)
        quant_c(0)
        stage2(0)
        widen(3)

        for n in range(1, UNITS + 1):
            last = n - 1 >= UNITS - 2
            stage1(n)
            turn(n + 2)
            if last:
                take_plain(n - 1, 1)
            else:
                take_all(n - 1, 1)
            take_plain(n - 1, 0)
            scale_x(n + 1, 0)
            products(n - 1, 0, nc.vector, live["qt", n - 1, 0][:])
            if last:
                products(n - 1, 1, nc.vector, live["qt", n - 1, 1][:])
            else:
                products(n - 1, 1, nc.gpsimd, live["ot", n - 1][:, 1, :])
            gather_cq(n, 0, nc.scalar.copy)
            gather_cq(n, 1, nc.scalar.copy)
            scale_x(n + 1, 1)
            widen(n + 3)
            sums(n - 1, 1, nc.vector if last else nc.gpsimd)
            sums(n - 1, 0, nc.gpsimd)
            store(n - 1)
            quant_c(n)
            quant_x(n + 1)
            stage2(n)
